import numpy as np
import ml_dtypes


def mxq(x, axis, fmt="e4m3"):
    dtype, down = {"e4m3": (ml_dtypes.float8_e4m3fn, 7), "e5m2": (ml_dtypes.float8_e5m2, 14)}[fmt]
    v = np.moveaxis(np.asarray(x, np.float32).astype(ml_dtypes.bfloat16).astype(np.float64), axis, -1)
    blocks = v.reshape(v.shape[:-1] + (-1, 32))
    amax = np.abs(blocks).max(-1, keepdims=True)
    byte = np.maximum(np.where(amax > 0, np.frexp(amax)[1] - 1 + 127, 0) - down, 1)
    scale = np.exp2(byte - 127.0)
    codes = (blocks / scale).astype(np.float32).astype(dtype).astype(np.float64)
    return np.moveaxis((codes * scale).reshape(v.shape), -1, axis)


WIDE = False


def mx_kscale(k):
    if not WIDE:
        return np.ones(k)
    levels = np.array([20, -20, 10, -10, 0])
    a = np.random.permutation(np.resize(levels, k // 512 * 4)).reshape(k // 512, 4)
    idx = np.arange(k)
    return np.exp2(a[idx // 512, idx % 128 // 32])


BF16 = ml_dtypes.bfloat16


def bf(x):
    return np.asarray(x, np.float32).astype(BF16)


def f64(x):
    return np.asarray(x).astype(np.float64)


N, I, O = 4096, 1024, 1024
THRESHOLD = 0.05


def binarize101(w, threshold):
    pos = (w > threshold).astype(np.float64)
    neg = (w < -threshold).astype(np.float64)
    return pos - neg


def setup_inputs():
    s = mx_kscale(O)
    r = s / s.min()
    c = np.sqrt(O / np.sum(r == 1.0))
    x = np.random.standard_normal((N, I)) * 2.0 / np.sqrt(I)
    weight = np.random.standard_normal((O, I)) * 0.1 / r[:, None]
    bias = np.random.standard_normal(O)
    g = np.random.standard_normal((N, O)) * np.exp2(np.random.randint(-12, 1, (N, 1))) * r * c
    return {"x": bf(x), "weight": bf(weight), "bias": bf(bias), "grad_out": bf(g)}


def reference(x, weight, bias, grad_out):
    wb = binarize101(f64(weight), THRESHOLD)
    return mxq(f64(grad_out), 1, "e5m2") @ mxq(wb, 0, "e4m3")

@@ -1,0 +1,212 @@
+from contextlib import ExitStack
+
+import concourse.mybir as mybir
+from concourse.masks import make_identity
+
+F32 = mybir.dt.float32
+BF16 = mybir.dt.bfloat16
+U32 = mybir.dt.uint32
+U8 = mybir.dt.uint8
+E4X4 = mybir.dt.float8_e4m3fn_x4
+E5X4 = mybir.dt.float8_e5m2_x4
+ALU = mybir.AluOpType
+
+P = 128
+N_TOK, N_OUT, N_IN = 4096, 1024, 1024
+THRESHOLD = 0.05
+FLOPS = 2 * N_TOK * N_OUT * N_IN
+BYTES = 2 * N_TOK * N_OUT + 2 * N_OUT * N_IN + 4 * N_TOK * N_IN
+
+N_TILES = N_TOK // P
+HALF = 512
+SIZES = [2, 2, 4, 4, 4, 4, 4, 4, 4]
+HEAD = 3
+
+
+def tile_linearbin_t_kernel(tc, x, weight, bias, grad_out, out):
+    nc = tc.nc
+    n_bunch = len(SIZES)
+    first = [sum(SIZES[:b]) for b in range(n_bunch)]
+    g_view = grad_out.rearrange("(p t) k -> p (t k)", t=N_TILES)
+    o_view = out.rearrange("(p t) i -> p (t i)", t=N_TILES)
+
+    with ExitStack() as ctx:
+        const = ctx.enter_context(tc.tile_pool(name="const", bufs=1))
+        negp = ctx.enter_context(tc.tile_pool(name="negp", bufs=2))
+        grawp = ctx.enter_context(tc.tile_pool(name="grawp", bufs=6))
+        grpp = ctx.enter_context(tc.tile_pool(name="grpp", bufs=2))
+        gqp = ctx.enter_context(tc.tile_pool(name="gqp", bufs=5))
+        osp = ctx.enter_context(tc.tile_pool(name="osp", bufs=9))
+        xtp = ctx.enter_context(tc.psum_pool(name="xtp", bufs=4))
+        accp = ctx.enter_context(tc.psum_pool(name="accp", bufs=4))
+        ctx.enter_context(tc.manual_schedule())
+
+        ident = const.tile([P, P], F32, name="ident")
+        make_identity(nc, ident[:])
+
+        wraw = [const.tile([P, 2, 2, N_IN], BF16, name="wraw%d" % g) for g in range(2)]
+        wbg = {}
+        wq = {}
+        ws = {}
+        for g in range(2):
+            for h in range(2):
+                wbg[(g, h)] = const.tile([P, HALF, 4], BF16, name="wbg%d%d" % (g, h), align_bytes=64)
+                wq[(g, h)] = const.tile([P, HALF], U32, name="wq%d%d" % (g, h), align_bytes=64)
+                ws[(g, h)] = const.tile([P, HALF], U8, name="ws%d%d" % (g, h), align_bytes=64)
+
+        graw = {}
+        grp = {}
+        gq = {}
+        gs = {}
+        xts = {}
+        ost = {}
+
+        def load_w(g):
+            nc.sync.dma_start(
+                out=wraw[g][:],
+                in_=weight[512 * g : 512 * (g + 1), :].rearrange("(u q e) c -> q u e c", u=2, e=2),
+            )
+
+        def load_g(b):
+            nt = SIZES[b]
+            graw[b] = grawp.tile([P, nt * N_OUT], BF16, name="graw", tag="graw")
+            nc.sync.dma_start(out=graw[b][:], in_=g_view[:, first[b] * N_OUT : (first[b] + nt) * N_OUT])
+
+        def prep_w(g, h):
+            wv = wraw[g][:].rearrange("p u e c -> p (u e) c")[:, :, HALF * h : HALF * (h + 1)]
+            neg = negp.tile([P, 4, HALF], BF16, name="neg", tag="neg")
+            nc.vector.tensor_scalar(out=neg[:], in0=wv, scalar1=-THRESHOLD, scalar2=None, op0=ALU.is_lt)
+            nc.vector.scalar_tensor_tensor(
+                out=wbg[(g, h)][:],
+                in0=wv.rearrange("p t c -> p c t"),
+                scalar=THRESHOLD,
+                in1=neg[:].rearrange("p t c -> p c t"),
+                op0=ALU.is_gt,
+                op1=ALU.subtract,
+            )
+
+        def quant_w(g, h):
+            nc.vector.quantize_mx(
+                out=wq[(g, h)][:].bitcast(E4X4),
+                scales=ws[(g, h)][:],
+                in_=wbg[(g, h)][:].rearrange("p c t -> p (c t)"),
+            )
+
+        def transposes(b):
+            g32 = graw[b][:].bitcast(F32)
+            for i in range(SIZES[b]):
+                xt = xtp.tile([P, 4, P], F32, name="xt", tag="xt")
+                for s in range(4):
+                    c0 = 512 * i + P * s
+                    nc.tensor.transpose(xt[:, s, :], g32[:, c0 : c0 + P], ident[:])
+                xts[(b, i)] = xt
+
+        def copy_t(b, i, on_vector):
+            nt = SIZES[b]
+            if i == 0:
+                grp[b] = grpp.tile([P, nt * N_OUT], BF16, name="grp", tag="grp", align_bytes=64)
+            dst = grp[b][:].bitcast(F32).rearrange("p (i g r u) -> p i g r u", i=nt, g=2, u=2)[:, i]
+            src = xts[(b, i)][:].rearrange("p (g u) r -> p g r u", u=2)
+            if on_vector:
+                nc.vector.tensor_copy(out=dst, in_=src)
+            else:
+                nc.scalar.copy(out=dst, in_=src)
+
+        def quant_g(b):
+            nt = SIZES[b]
+            gq[b] = gqp.tile([P, nt * 256], U32, name="gq", tag="gq", align_bytes=64)
+            gs[b] = gqp.tile([P, nt * 256], U8, name="gs", tag="gs", align_bytes=64)
+            nc.vector.quantize_mx(out=gq[b][:].bitcast(E5X4), scales=gs[b][:], in_=grp[b][:])
+
+        def group(b, i, h, on_vector):
+            acc = accp.tile([P, HALF], F32, name="acc", tag="acc")
+            for g in range(2):
+                c0 = (2 * i + g) * P
+                nc.tensor.matmul_mx(
+                    out=acc[:],
+                    lhsT=gq[b][:, c0 : c0 + P].bitcast(E5X4),
+                    lhsT_scale=gs[b][:, c0 : c0 + P],
+                    rhs=wq[(g, h)][:].bitcast(E4X4),
+                    rhs_scale=ws[(g, h)][:],
+                    start=(g == 0),
+                    stop=(g == 1),
+                )
+            t = first[b] + i
+            if t // 2 not in ost:
+                ost[t // 2] = osp.tile([P, 2 * N_IN], F32, name="ost", tag="ost")
+            c0 = (t % 2) * N_IN + h * HALF
+            dst = ost[t // 2][:, c0 : c0 + HALF]
+            if on_vector:
+                nc.vector.tensor_copy(out=dst, in_=acc[:])
+            else:
+                nc.scalar.copy(out=dst, in_=acc[:])
+
+        def store(t, c0, width):
+            nc.sync.dma_start(out=o_view[:, t * N_IN + c0 : t * N_IN + c0 + width], in_=ost[t // 2][:, c0 : c0 + width])
+
+        load_w(0)
+        load_g(0)
+        load_w(1)
+        for b in range(1, 6):
+            load_g(b)
+        prep_w(0, 0)
+        transposes(0)
+        load_g(6)
+        copy_t(0, 0, False)
+        copy_t(0, 1, False)
+        quant_g(0)
+        prep_w(1, 0)
+        transposes(1)
+        load_g(7)
+        copy_t(1, 0, False)
+        copy_t(1, 1, False)
+        quant_w(0, 0)
+        quant_w(1, 0)
+        quant_g(1)
+        transposes(2)
+        load_g(8)
+        for i in range(4):
+            copy_t(2, i, False)
+        prep_w(0, 1)
+        for b in range(2):
+            for i in range(SIZES[b]):
+                group(b, i, 0, False)
+        quant_g(2)
+        prep_w(1, 1)
+        for i in range(4):
+            group(2, i, 0, False)
+        transposes(3)
+        for i in range(4):
+            copy_t(3, i, False)
+        quant_w(0, 1)
+        quant_w(1, 1)
+        quant_g(3)
+        n = 0
+        for b in range(HEAD):
+            for i in range(SIZES[b]):
+                group(b, i, 1, n % 2 == 0)
+                n += 1
+                if i % 2 == 1:
+                    store(first[b] + i - 1, 0, 2 * N_IN)
+
+        for b in range(HEAD, n_bunch):
+            last = b == n_bunch - 1
+            if not last:
+                transposes(b + 1)
+                for i in range(4):
+                    copy_t(b + 1, i, i >= 2)
+            for n in range(8):
+                i, h = divmod(n, 2)
+                t = first[b] + i
+                if last:
+                    group(b, i, h, n % 2 == 1)
+                    if i == 3:
+                        store(t - 1, N_IN + h * HALF, HALF)
+                    elif h == 1:
+                        store(t - t % 2, (t % 2) * N_IN, N_IN)
+                else:
+                    group(b, i, h, n in (0, 3, 7))
+                    if n == 1:
+                        quant_g(b + 1)
+                    if n in (3, 7):
+                        store(t - 1, 0, 2 * N_IN)

@@ -10,6 +10,7 @@ U8 = mybir.dt.uint8
 E4X4 = mybir.dt.float8_e4m3fn_x4
 E5X4 = mybir.dt.float8_e5m2_x4
 ALU = mybir.AluOpType
+ACT = mybir.ActivationFunctionType
 
 P = 128
 N_TOK, N_OUT, N_IN = 4096, 1024, 1024
@@ -20,6 +21,7 @@ BYTES = 2 * N_TOK * N_OUT + 2 * N_OUT * N_IN + 4 * N_TOK * N_IN
 N_TILES = N_TOK // P
 HALF = 512
 SIZES = [2, 2, 4, 4, 4, 4, 4, 4, 4]
+FINE = 6
 HEAD = 3
 
 
@@ -32,7 +34,6 @@ def tile_linearbin_t_kernel(tc, x, weight, bias, grad_out, out):
 
     with ExitStack() as ctx:
         const = ctx.enter_context(tc.tile_pool(name="const", bufs=1))
-        negp = ctx.enter_context(tc.tile_pool(name="negp", bufs=2))
         grawp = ctx.enter_context(tc.tile_pool(name="grawp", bufs=6))
         grpp = ctx.enter_context(tc.tile_pool(name="grpp", bufs=2))
         gqp = ctx.enter_context(tc.tile_pool(name="gqp", bufs=5))
@@ -45,11 +46,15 @@ def tile_linearbin_t_kernel(tc, x, weight, bias, grad_out, out):
         make_identity(nc, ident[:])
 
         wraw = [const.tile([P, 2, 2, N_IN], BF16, name="wraw%d" % g) for g in range(2)]
+        thr = const.tile([P, 1], F32, name="thr")
+        nc.vector.memset(thr[:], THRESHOLD)
+        low = {}
         wbg = {}
         wq = {}
         ws = {}
         for g in range(2):
             for h in range(2):
+                low[(g, h)] = const.tile([P, 4, HALF], BF16, name="low%d%d" % (g, h))
                 wbg[(g, h)] = const.tile([P, HALF, 4], BF16, name="wbg%d%d" % (g, h), align_bytes=64)
                 wq[(g, h)] = const.tile([P, HALF], U32, name="wq%d%d" % (g, h), align_bytes=64)
                 ws[(g, h)] = const.tile([P, HALF], U8, name="ws%d%d" % (g, h), align_bytes=64)
@@ -72,17 +77,27 @@ def tile_linearbin_t_kernel(tc, x, weight, bias, grad_out, out):
             graw[b] = grawp.tile([P, nt * N_OUT], BF16, name="graw", tag="graw")
             nc.sync.dma_start(out=graw[b][:], in_=g_view[:, first[b] * N_OUT : (first[b] + nt) * N_OUT])
 
-        def prep_w(g, h):
-            wv = wraw[g][:].rearrange("p u e c -> p (u e) c")[:, :, HALF * h : HALF * (h + 1)]
-            neg = negp.tile([P, 4, HALF], BF16, name="neg", tag="neg")
-            nc.vector.tensor_scalar(out=neg[:], in0=wv, scalar1=-THRESHOLD, scalar2=None, op0=ALU.is_lt)
+        def w_view(g, h, c0, c1):
+            return wraw[g][:].rearrange("p u e c -> p (u e) c")[:, :, HALF * h + c0 : HALF * h + c1]
+
+        def low_v(g, h):
+            nc.vector.tensor_scalar(
+                out=low[(g, h)][:], in0=w_view(g, h, 0, HALF), scalar1=-THRESHOLD, scalar2=None, op0=ALU.is_lt
+            )
+
+        def low_s(g, h, c0, c1):
+            nc.scalar.activation(
+                out=low[(g, h)][:, :, c0:c1], in_=w_view(g, h, c0, c1), func=ACT.Sign, bias=thr[:, 0:1], scale=1.0
+            )
+
+        def ternary(g, h, c0, c1, op1):
             nc.vector.scalar_tensor_tensor(
-                out=wbg[(g, h)][:],
-                in0=wv.rearrange("p t c -> p c t"),
+                out=wbg[(g, h)][:, c0:c1, :],
+                in0=w_view(g, h, c0, c1).rearrange("p t c -> p c t"),
                 scalar=THRESHOLD,
-                in1=neg[:].rearrange("p t c -> p c t"),
+                in1=low[(g, h)][:, :, c0:c1].rearrange("p t c -> p c t"),
                 op0=ALU.is_gt,
-                op1=ALU.subtract,
+                op1=op1,
             )
 
         def quant_w(g, h):
@@ -144,22 +159,29 @@ def tile_linearbin_t_kernel(tc, x, weight, bias, grad_out, out):
         def store(t, c0, width):
             nc.sync.dma_start(out=o_view[:, t * N_IN + c0 : t * N_IN + c0 + width], in_=ost[t // 2][:, c0 : c0 + width])
 
+        Q = HALF // 2
         load_w(0)
         load_g(0)
         load_w(1)
         for b in range(1, 6):
             load_g(b)
-        prep_w(0, 0)
+        low_v(0, 0)
+        ternary(0, 0, 0, HALF, ALU.subtract)
+        low_s(0, 1, 0, Q)
         transposes(0)
         load_g(6)
         copy_t(0, 0, False)
         copy_t(0, 1, False)
+        low_s(0, 1, Q, HALF)
         quant_g(0)
-        prep_w(1, 0)
+        low_v(1, 0)
+        ternary(1, 0, 0, HALF, ALU.subtract)
+        low_s(1, 1, 0, Q)
         transposes(1)
         load_g(7)
         copy_t(1, 0, False)
         copy_t(1, 1, False)
+        low_s(1, 1, Q, HALF)
         quant_w(0, 0)
         quant_w(1, 0)
         quant_g(1)
@@ -167,25 +189,27 @@ def tile_linearbin_t_kernel(tc, x, weight, bias, grad_out, out):
         load_g(8)
         for i in range(4):
             copy_t(2, i, False)
-        prep_w(0, 1)
         for b in range(2):
             for i in range(SIZES[b]):
                 group(b, i, 0, False)
+        ternary(0, 1, 0, Q, ALU.min)
         quant_g(2)
-        prep_w(1, 1)
+        ternary(0, 1, Q, HALF, ALU.min)
         for i in range(4):
             group(2, i, 0, False)
         transposes(3)
-        for i in range(4):
-            copy_t(3, i, False)
+        ternary(1, 1, 0, HALF, ALU.min)
         quant_w(0, 1)
         quant_w(1, 1)
-        quant_g(3)
+        for i in range(4):
+            copy_t(3, i, False)
         n = 0
         for b in range(HEAD):
             for i in range(SIZES[b]):
                 group(b, i, 1, n % 2 == 0)
                 n += 1
+                if n == 4:
+                    quant_g(3)
                 if i % 2 == 1:
                     store(first[b] + i - 1, 0, 2 * N_IN)
 
@@ -198,15 +222,13 @@ def tile_linearbin_t_kernel(tc, x, weight, bias, grad_out, out):
             for n in range(8):
                 i, h = divmod(n, 2)
                 t = first[b] + i
-                if last:
-                    group(b, i, h, n % 2 == 1)
-                    if i == 3:
-                        store(t - 1, N_IN + h * HALF, HALF)
-                    elif h == 1:
+                group(b, i, h, n % 2 == 1 if last else n in (0, 3, 7))
+                if n == 1 and not last:
+                    quant_g(b + 1)
+                if last and i == 3:
+                    store(t - 1, N_IN + h * HALF, HALF)
+                elif b >= FINE:
+                    if h == 1:
                         store(t - t % 2, (t % 2) * N_IN, N_IN)
-                else:
-                    group(b, i, h, n in (0, 3, 7))
-                    if n == 1:
-                        quant_g(b + 1)
-                    if n in (3, 7):
-                        store(t - 1, 0, 2 * N_IN)
+                elif n in (3, 7):
+                    store(t - 1, 0, 2 * N_IN)

@@ -21,6 +21,7 @@ BYTES = 2 * N_TOK * N_OUT + 2 * N_OUT * N_IN + 4 * N_TOK * N_IN
 N_TILES = N_TOK // P
 HALF = 512
 SIZES = [2, 2, 4, 4, 4, 4, 4, 4, 4]
+SPLIT = 336
 FINE = 6
 HEAD = 3
 
@@ -133,28 +134,37 @@ def tile_linearbin_t_kernel(tc, x, weight, bias, grad_out, out):
             gs[b] = gqp.tile([P, nt * 256], U8, name="gs", tag="gs", align_bytes=64)
             nc.vector.quantize_mx(out=gq[b][:].bitcast(E5X4), scales=gs[b][:], in_=grp[b][:])
 
-        def group(b, i, h, on_vector):
-            acc = accp.tile([P, HALF], F32, name="acc", tag="acc")
-            for g in range(2):
-                c0 = (2 * i + g) * P
-                nc.tensor.matmul_mx(
-                    out=acc[:],
-                    lhsT=gq[b][:, c0 : c0 + P].bitcast(E5X4),
-                    lhsT_scale=gs[b][:, c0 : c0 + P],
-                    rhs=wq[(g, h)][:].bitcast(E4X4),
-                    rhs_scale=ws[(g, h)][:],
-                    start=(g == 0),
-                    stop=(g == 1),
-                )
+        accs = {}
+
+        def mx_pass(b, i, h, g):
+            if g == 0:
+                accs[(b, i, h)] = accp.tile([P, HALF], F32, name="acc", tag="acc")
+            c0 = (2 * i + g) * P
+            nc.tensor.matmul_mx(
+                out=accs[(b, i, h)][:],
+                lhsT=gq[b][:, c0 : c0 + P].bitcast(E5X4),
+                lhsT_scale=gs[b][:, c0 : c0 + P],
+                rhs=wq[(g, h)][:].bitcast(E4X4),
+                rhs_scale=ws[(g, h)][:],
+                start=(g == 0),
+                stop=(g == 1),
+            )
+
+        def evacuate(b, i, h, on_vector):
             t = first[b] + i
             if t // 2 not in ost:
                 ost[t // 2] = osp.tile([P, 2 * N_IN], F32, name="ost", tag="ost")
             c0 = (t % 2) * N_IN + h * HALF
             dst = ost[t // 2][:, c0 : c0 + HALF]
             if on_vector:
-                nc.vector.tensor_copy(out=dst, in_=acc[:])
+                nc.vector.tensor_copy(out=dst, in_=accs[(b, i, h)][:])
             else:
-                nc.scalar.copy(out=dst, in_=acc[:])
+                nc.scalar.copy(out=dst, in_=accs[(b, i, h)][:])
+
+        def group(b, i, h, on_vector):
+            mx_pass(b, i, h, 0)
+            mx_pass(b, i, h, 1)
+            evacuate(b, i, h, on_vector)
 
         def store(t, c0, width):
             nc.sync.dma_start(out=o_view[:, t * N_IN + c0 : t * N_IN + c0 + width], in_=ost[t // 2][:, c0 : c0 + width])
@@ -192,38 +202,43 @@ def tile_linearbin_t_kernel(tc, x, weight, bias, grad_out, out):
         for b in range(2):
             for i in range(SIZES[b]):
                 group(b, i, 0, False)
-        ternary(0, 1, 0, Q, ALU.min)
+        ternary(0, 1, 0, SPLIT, ALU.min)
         quant_g(2)
-        ternary(0, 1, Q, HALF, ALU.min)
+        ternary(0, 1, SPLIT, HALF, ALU.min)
         for i in range(4):
             group(2, i, 0, False)
         transposes(3)
-        ternary(1, 1, 0, HALF, ALU.min)
         quant_w(0, 1)
+        ternary(1, 1, 0, HALF, ALU.min)
+        early = [(0, 0), (0, 1), (1, 0), (1, 1)]
+        for b, i in early:
+            mx_pass(b, i, 1, 0)
         quant_w(1, 1)
         for i in range(4):
             copy_t(3, i, False)
-        n = 0
-        for b in range(HEAD):
-            for i in range(SIZES[b]):
-                group(b, i, 1, n % 2 == 0)
-                n += 1
-                if n == 4:
-                    quant_g(3)
-                if i % 2 == 1:
-                    store(first[b] + i - 1, 0, 2 * N_IN)
+        for b, i in early:
+            mx_pass(b, i, 1, 1)
+            evacuate(b, i, 1, i == 1)
+            if i == 1:
+                store(first[b], 0, 2 * N_IN)
+        quant_g(3)
+        for i in range(4):
+            group(2, i, 1, i % 2 == 1)
+            if i % 2 == 1:
+                store(first[2] + i - 1, 0, 2 * N_IN)
 
         for b in range(HEAD, n_bunch):
             last = b == n_bunch - 1
-            if not last:
-                transposes(b + 1)
-                for i in range(4):
-                    copy_t(b + 1, i, i >= 2)
+            t_at = 2 if b == n_bunch - 2 else 0
             for n in range(8):
                 i, h = divmod(n, 2)
                 t = first[b] + i
+                if n == t_at and not last:
+                    transposes(b + 1)
+                    for j in range(4):
+                        copy_t(b + 1, j, j >= 2)
                 group(b, i, h, n % 2 == 1 if last else n in (0, 3, 7))
-                if n == 1 and not last:
+                if n == t_at + 1 and not last:
                     quant_g(b + 1)
                 if last and i == 3:
                     store(t - 1, N_IN + h * HALF, HALF)

@@ -49,6 +49,9 @@ def tile_linearbin_t_kernel(tc, x, weight, bias, grad_out, out):
         wraw = [const.tile([P, 2, 2, N_IN], BF16, name="wraw%d" % g) for g in range(2)]
         thr = const.tile([P, 1], F32, name="thr")
         nc.vector.memset(thr[:], THRESHOLD)
+        zeros = const.tile([P, HALF // 2], F32, name="zeros")
+        nc.vector.memset(zeros[:], 0.0)
+        warm = zeros[:].bitcast(BF16)
         low = {}
         wbg = {}
         wq = {}
@@ -108,9 +111,16 @@ def tile_linearbin_t_kernel(tc, x, weight, bias, grad_out, out):
                 in_=wbg[(g, h)][:].rearrange("p c t -> p (c t)"),
             )
 
-        def transposes(b):
+        def warm_up(count):
+            scrap = accp.tile([P, HALF], F32, name="acc", tag="acc")
+            for k in range(count):
+                nc.tensor.matmul(out=scrap[:], lhsT=warm[:, 0:P], rhs=warm, start=True, stop=True)
+
+        def transposes(b, pause=0):
             g32 = graw[b][:].bitcast(F32)
             for i in range(SIZES[b]):
+                if pause and i == 2:
+                    warm_up(pause)
                 xt = xtp.tile([P, 4, P], F32, name="xt", tag="xt")
                 for s in range(4):
                     c0 = 512 * i + P * s
@@ -179,6 +189,7 @@ def tile_linearbin_t_kernel(tc, x, weight, bias, grad_out, out):
         ternary(0, 0, 0, HALF, ALU.subtract)
         low_s(0, 1, 0, Q)
         transposes(0)
+        warm_up(3)
         load_g(6)
         copy_t(0, 0, False)
         copy_t(0, 1, False)
@@ -188,6 +199,7 @@ def tile_linearbin_t_kernel(tc, x, weight, bias, grad_out, out):
         ternary(1, 0, 0, HALF, ALU.subtract)
         low_s(1, 1, 0, Q)
         transposes(1)
+        warm_up(3)
         load_g(7)
         copy_t(1, 0, False)
         copy_t(1, 1, False)
@@ -195,7 +207,7 @@ def tile_linearbin_t_kernel(tc, x, weight, bias, grad_out, out):
         quant_w(0, 0)
         quant_w(1, 0)
         quant_g(1)
-        transposes(2)
+        transposes(2, 2)
         load_g(8)
         for i in range(4):
             copy_t(2, i, False)

@@ -21,7 +21,7 @@ BYTES = 2 * N_TOK * N_OUT + 2 * N_OUT * N_IN + 4 * N_TOK * N_IN
 N_TILES = N_TOK // P
 HALF = 512
 SIZES = [2, 2, 4, 4, 4, 4, 4, 4, 4]
-SPLIT = 336
+PAD = 48
 FINE = 6
 HEAD = 3
 
@@ -49,9 +49,6 @@ def tile_linearbin_t_kernel(tc, x, weight, bias, grad_out, out):
         wraw = [const.tile([P, 2, 2, N_IN], BF16, name="wraw%d" % g) for g in range(2)]
         thr = const.tile([P, 1], F32, name="thr")
         nc.vector.memset(thr[:], THRESHOLD)
-        zeros = const.tile([P, HALF // 2], F32, name="zeros")
-        nc.vector.memset(zeros[:], 0.0)
-        warm = zeros[:].bitcast(BF16)
         low = {}
         wbg = {}
         wq = {}
@@ -60,8 +57,8 @@ def tile_linearbin_t_kernel(tc, x, weight, bias, grad_out, out):
             for h in range(2):
                 low[(g, h)] = const.tile([P, 4, HALF], BF16, name="low%d%d" % (g, h))
                 wbg[(g, h)] = const.tile([P, HALF, 4], BF16, name="wbg%d%d" % (g, h), align_bytes=64)
-                wq[(g, h)] = const.tile([P, HALF], U32, name="wq%d%d" % (g, h), align_bytes=64)
-                ws[(g, h)] = const.tile([P, HALF], U8, name="ws%d%d" % (g, h), align_bytes=64)
+                wq[(g, h)] = const.tile([P, HALF], U32, name="wq%d%d" % (g, h), align_bytes=256)
+                ws[(g, h)] = const.tile([P, HALF], U8, name="ws%d%d" % (g, h), align_bytes=256)
 
         graw = {}
         grp = {}
@@ -111,16 +108,9 @@ def tile_linearbin_t_kernel(tc, x, weight, bias, grad_out, out):
                 in_=wbg[(g, h)][:].rearrange("p c t -> p (c t)"),
             )
 
-        def warm_up(count):
-            scrap = accp.tile([P, HALF], F32, name="acc", tag="acc")
-            for k in range(count):
-                nc.tensor.matmul(out=scrap[:], lhsT=warm[:, 0:P], rhs=warm, start=True, stop=True)
-
-        def transposes(b, pause=0):
+        def transposes(b):
             g32 = graw[b][:].bitcast(F32)
             for i in range(SIZES[b]):
-                if pause and i == 2:
-                    warm_up(pause)
                 xt = xtp.tile([P, 4, P], F32, name="xt", tag="xt")
                 for s in range(4):
                     c0 = 512 * i + P * s
@@ -140,41 +130,32 @@ def tile_linearbin_t_kernel(tc, x, weight, bias, grad_out, out):
 
         def quant_g(b):
             nt = SIZES[b]
-            gq[b] = gqp.tile([P, nt * 256], U32, name="gq", tag="gq", align_bytes=64)
-            gs[b] = gqp.tile([P, nt * 256], U8, name="gs", tag="gs", align_bytes=64)
-            nc.vector.quantize_mx(out=gq[b][:].bitcast(E5X4), scales=gs[b][:], in_=grp[b][:])
+            gq[b] = gqp.tile([P, PAD + nt * 256], U32, name="gq", tag="gq", align_bytes=256)
+            gs[b] = gqp.tile([P, nt * 256], U8, name="gs", tag="gs", align_bytes=256)
+            nc.vector.quantize_mx(out=gq[b][:, PAD:].bitcast(E5X4), scales=gs[b][:], in_=grp[b][:])
 
-        accs = {}
-
-        def mx_pass(b, i, h, g):
-            if g == 0:
-                accs[(b, i, h)] = accp.tile([P, HALF], F32, name="acc", tag="acc")
-            c0 = (2 * i + g) * P
-            nc.tensor.matmul_mx(
-                out=accs[(b, i, h)][:],
-                lhsT=gq[b][:, c0 : c0 + P].bitcast(E5X4),
-                lhsT_scale=gs[b][:, c0 : c0 + P],
-                rhs=wq[(g, h)][:].bitcast(E4X4),
-                rhs_scale=ws[(g, h)][:],
-                start=(g == 0),
-                stop=(g == 1),
-            )
-
-        def evacuate(b, i, h, on_vector):
+        def group(b, i, h, on_vector):
+            acc = accp.tile([P, HALF], F32, name="acc", tag="acc")
+            for g in range(2):
+                c0 = (2 * i + g) * P
+                nc.tensor.matmul_mx(
+                    out=acc[:],
+                    lhsT=gq[b][:, PAD + c0 : PAD + c0 + P].bitcast(E5X4),
+                    lhsT_scale=gs[b][:, c0 : c0 + P],
+                    rhs=wq[(g, h)][:].bitcast(E4X4),
+                    rhs_scale=ws[(g, h)][:],
+                    start=(g == 0),
+                    stop=(g == 1),
+                )
             t = first[b] + i
             if t // 2 not in ost:
                 ost[t // 2] = osp.tile([P, 2 * N_IN], F32, name="ost", tag="ost")
             c0 = (t % 2) * N_IN + h * HALF
             dst = ost[t // 2][:, c0 : c0 + HALF]
             if on_vector:
-                nc.vector.tensor_copy(out=dst, in_=accs[(b, i, h)][:])
+                nc.vector.tensor_copy(out=dst, in_=acc[:])
             else:
-                nc.scalar.copy(out=dst, in_=accs[(b, i, h)][:])
-
-        def group(b, i, h, on_vector):
-            mx_pass(b, i, h, 0)
-            mx_pass(b, i, h, 1)
-            evacuate(b, i, h, on_vector)
+                nc.scalar.copy(out=dst, in_=acc[:])
 
         def store(t, c0, width):
             nc.sync.dma_start(out=o_view[:, t * N_IN + c0 : t * N_IN + c0 + width], in_=ost[t // 2][:, c0 : c0 + width])
@@ -189,7 +170,6 @@ def tile_linearbin_t_kernel(tc, x, weight, bias, grad_out, out):
         ternary(0, 0, 0, HALF, ALU.subtract)
         low_s(0, 1, 0, Q)
         transposes(0)
-        warm_up(3)
         load_g(6)
         copy_t(0, 0, False)
         copy_t(0, 1, False)
@@ -199,7 +179,6 @@ def tile_linearbin_t_kernel(tc, x, weight, bias, grad_out, out):
         ternary(1, 0, 0, HALF, ALU.subtract)
         low_s(1, 1, 0, Q)
         transposes(1)
-        warm_up(3)
         load_g(7)
         copy_t(1, 0, False)
         copy_t(1, 1, False)
@@ -207,50 +186,45 @@ def tile_linearbin_t_kernel(tc, x, weight, bias, grad_out, out):
         quant_w(0, 0)
         quant_w(1, 0)
         quant_g(1)
-        transposes(2, 2)
+        transposes(2)
         load_g(8)
         for i in range(4):
             copy_t(2, i, False)
         for b in range(2):
             for i in range(SIZES[b]):
                 group(b, i, 0, False)
-        ternary(0, 1, 0, SPLIT, ALU.min)
+        ternary(0, 1, 0, Q, ALU.min)
         quant_g(2)
-        ternary(0, 1, SPLIT, HALF, ALU.min)
+        ternary(0, 1, Q, HALF, ALU.min)
         for i in range(4):
             group(2, i, 0, False)
         transposes(3)
-        quant_w(0, 1)
         ternary(1, 1, 0, HALF, ALU.min)
-        early = [(0, 0), (0, 1), (1, 0), (1, 1)]
-        for b, i in early:
-            mx_pass(b, i, 1, 0)
+        quant_w(0, 1)
         quant_w(1, 1)
         for i in range(4):
             copy_t(3, i, False)
-        for b, i in early:
-            mx_pass(b, i, 1, 1)
-            evacuate(b, i, 1, i == 1)
-            if i == 1:
-                store(first[b], 0, 2 * N_IN)
-        quant_g(3)
-        for i in range(4):
-            group(2, i, 1, i % 2 == 1)
-            if i % 2 == 1:
-                store(first[2] + i - 1, 0, 2 * N_IN)
+        n = 0
+        for b in range(HEAD):
+            for i in range(SIZES[b]):
+                group(b, i, 1, n % 2 == 0)
+                n += 1
+                if n == 4:
+                    quant_g(3)
+                if i % 2 == 1:
+                    store(first[b] + i - 1, 0, 2 * N_IN)
 
         for b in range(HEAD, n_bunch):
             last = b == n_bunch - 1
-            t_at = 2 if b == n_bunch - 2 else 0
+            if not last:
+                transposes(b + 1)
+                for i in range(4):
+                    copy_t(b + 1, i, i >= 2)
             for n in range(8):
                 i, h = divmod(n, 2)
                 t = first[b] + i
-                if n == t_at and not last:
-                    transposes(b + 1)
-                    for j in range(4):
-                        copy_t(b + 1, j, j >= 2)
                 group(b, i, h, n % 2 == 1 if last else n in (0, 3, 7))
-                if n == t_at + 1 and not last:
+                if n == 1 and not last:
                     quant_g(b + 1)
                 if last and i == 3:
                     store(t - 1, N_IN + h * HALF, HALF)

@@ -23,7 +23,7 @@ HALF = 512
 SIZES = [2, 2, 4, 4, 4, 4, 4, 4, 4]
 PAD = 48
 FINE = 6
-HEAD = 3
+HEAD = 5
 
 
 def tile_linearbin_t_kernel(tc, x, weight, bias, grad_out, out):
@@ -35,10 +35,10 @@ def tile_linearbin_t_kernel(tc, x, weight, bias, grad_out, out):
 
     with ExitStack() as ctx:
         const = ctx.enter_context(tc.tile_pool(name="const", bufs=1))
-        grawp = ctx.enter_context(tc.tile_pool(name="grawp", bufs=6))
+        grawp = ctx.enter_context(tc.tile_pool(name="grawp", bufs=7))
         grpp = ctx.enter_context(tc.tile_pool(name="grpp", bufs=2))
-        gqp = ctx.enter_context(tc.tile_pool(name="gqp", bufs=5))
-        osp = ctx.enter_context(tc.tile_pool(name="osp", bufs=9))
+        gqp = ctx.enter_context(tc.tile_pool(name="gqp", bufs=6))
+        osp = ctx.enter_context(tc.tile_pool(name="osp", bufs=4))
         xtp = ctx.enter_context(tc.psum_pool(name="xtp", bufs=4))
         accp = ctx.enter_context(tc.psum_pool(name="accp", bufs=4))
         ctx.enter_context(tc.manual_schedule())
@@ -49,14 +49,15 @@ def tile_linearbin_t_kernel(tc, x, weight, bias, grad_out, out):
         wraw = [const.tile([P, 2, 2, N_IN], BF16, name="wraw%d" % g) for g in range(2)]
         thr = const.tile([P, 1], F32, name="thr")
         nc.vector.memset(thr[:], THRESHOLD)
+        dummy = const.tile([P, 1], F32, name="dummy")
         low = {}
         wbg = {}
         wq = {}
         ws = {}
         for g in range(2):
             for h in range(2):
-                low[(g, h)] = const.tile([P, 4, HALF], BF16, name="low%d%d" % (g, h))
-                wbg[(g, h)] = const.tile([P, HALF, 4], BF16, name="wbg%d%d" % (g, h), align_bytes=64)
+                low[(g, h)] = const.tile([P, 4, HALF], BF16, name="low%d" % g)
+                wbg[(g, h)] = const.tile([P, HALF, 4], BF16, name="wbg%d" % g, align_bytes=64)
                 wq[(g, h)] = const.tile([P, HALF], U32, name="wq%d%d" % (g, h), align_bytes=256)
                 ws[(g, h)] = const.tile([P, HALF], U8, name="ws%d%d" % (g, h), align_bytes=256)
 
@@ -66,16 +67,20 @@ def tile_linearbin_t_kernel(tc, x, weight, bias, grad_out, out):
         gs = {}
         xts = {}
         ost = {}
+        osth = {}
+        accs = {}
 
-        def load_w(g):
-            nc.sync.dma_start(
-                out=wraw[g][:],
-                in_=weight[512 * g : 512 * (g + 1), :].rearrange("(u q e) c -> q u e c", u=2, e=2),
-            )
+        def load_w(g, h):
+            for u in range(2):
+                r0 = 512 * g + 256 * u
+                nc.sync.dma_start(
+                    out=wraw[g][:, u, :, HALF * h : HALF * (h + 1)],
+                    in_=weight[r0 : r0 + 256, HALF * h : HALF * (h + 1)].rearrange("(q e) c -> q e c", e=2),
+                )
 
         def load_g(b):
             nt = SIZES[b]
-            graw[b] = grawp.tile([P, nt * N_OUT], BF16, name="graw", tag="graw")
+            graw[b] = grawp.tile([P, nt * N_OUT], BF16, name="graw%d" % nt, tag="graw%d" % nt, bufs=2 if nt == 2 else 5)
             nc.sync.dma_start(out=graw[b][:], in_=g_view[:, first[b] * N_OUT : (first[b] + nt) * N_OUT])
 
         def w_view(g, h, c0, c1):
@@ -134,85 +139,126 @@ def tile_linearbin_t_kernel(tc, x, weight, bias, grad_out, out):
             gs[b] = gqp.tile([P, nt * 256], U8, name="gs", tag="gs", align_bytes=256)
             nc.vector.quantize_mx(out=gq[b][:, PAD:].bitcast(E5X4), scales=gs[b][:], in_=grp[b][:])
 
-        def group(b, i, h, on_vector):
-            acc = accp.tile([P, HALF], F32, name="acc", tag="acc")
-            for g in range(2):
-                c0 = (2 * i + g) * P
-                nc.tensor.matmul_mx(
-                    out=acc[:],
-                    lhsT=gq[b][:, PAD + c0 : PAD + c0 + P].bitcast(E5X4),
-                    lhsT_scale=gs[b][:, c0 : c0 + P],
-                    rhs=wq[(g, h)][:].bitcast(E4X4),
-                    rhs_scale=ws[(g, h)][:],
-                    start=(g == 0),
-                    stop=(g == 1),
-                )
+        def mx(b, i, h, g):
+            if g == 0:
+                accs[(b, i, h)] = accp.tile([P, HALF], F32, name="acc", tag="acc")
+            c0 = (2 * i + g) * P
+            nc.tensor.matmul_mx(
+                out=accs[(b, i, h)][:],
+                lhsT=gq[b][:, PAD + c0 : PAD + c0 + P].bitcast(E5X4),
+                lhsT_scale=gs[b][:, c0 : c0 + P],
+                rhs=wq[(g, h)][:].bitcast(E4X4),
+                rhs_scale=ws[(g, h)][:],
+                start=(g == 0),
+                stop=(g == 1),
+            )
+
+        def evacuate(b, i, h, on_vector):
             t = first[b] + i
-            if t // 2 not in ost:
-                ost[t // 2] = osp.tile([P, 2 * N_IN], F32, name="ost", tag="ost")
-            c0 = (t % 2) * N_IN + h * HALF
-            dst = ost[t // 2][:, c0 : c0 + HALF]
-            if on_vector:
-                nc.vector.tensor_copy(out=dst, in_=acc[:])
+            if b < HEAD:
+                if (t // 2, h) not in osth:
+                    osth[(t // 2, h)] = osp.tile([P, 2, HALF], F32, name="osth", tag="osth", bufs=12)
+                dst = osth[(t // 2, h)][:, t % 2, :]
             else:
-                nc.scalar.copy(out=dst, in_=acc[:])
+                if t // 2 not in ost:
+                    ost[t // 2] = osp.tile([P, 2 * N_IN], F32, name="ost", tag="ost")
+                c0 = (t % 2) * N_IN + h * HALF
+                dst = ost[t // 2][:, c0 : c0 + HALF]
+            src = accs[(b, i, h)][:]
+            if on_vector:
+                nc.vector.tensor_copy(out=dst, in_=src)
+            else:
+                nc.scalar.copy(out=dst, in_=src)
+
+        def group(b, i, h, on_vector):
+            mx(b, i, h, 0)
+            mx(b, i, h, 1)
+            evacuate(b, i, h, on_vector)
+
+        def store_half(t, h):
+            dst = o_view[:, t * N_IN : (t + 2) * N_IN].rearrange("p (t h i) -> p t h i", t=2, h=2)[:, :, h, :]
+            nc.sync.dma_start(out=dst, in_=osth[(t // 2, h)][:])
 
         def store(t, c0, width):
             nc.sync.dma_start(out=o_view[:, t * N_IN + c0 : t * N_IN + c0 + width], in_=ost[t // 2][:, c0 : c0 + width])
 
         Q = HALF // 2
-        load_w(0)
-        load_g(0)
-        load_w(1)
-        for b in range(1, 6):
+        load_w(0, 0)
+        load_w(1, 0)
+        for b in range(4):
             load_g(b)
+        load_w(0, 1)
+        load_w(1, 1)
+        for b in range(4, 7):
+            load_g(b)
+        nc.scalar.activation(out=dummy[:], in_=thr[:], func=ACT.Sign)
         low_v(0, 0)
         ternary(0, 0, 0, HALF, ALU.subtract)
-        low_s(0, 1, 0, Q)
-        transposes(0)
-        load_g(6)
-        copy_t(0, 0, False)
-        copy_t(0, 1, False)
-        low_s(0, 1, Q, HALF)
-        quant_g(0)
-        low_v(1, 0)
-        ternary(1, 0, 0, HALF, ALU.subtract)
-        low_s(1, 1, 0, Q)
-        transposes(1)
-        load_g(7)
-        copy_t(1, 0, False)
-        copy_t(1, 1, False)
-        low_s(1, 1, Q, HALF)
+        low_s(1, 0, 0, HALF)
         quant_w(0, 0)
-        quant_w(1, 0)
+        transposes(0)
+        transposes(1)
+        for b in range(2):
+            for i in range(2):
+                copy_t(b, i, False)
+        ternary(1, 0, 0, Q, ALU.min)
+        quant_g(0)
+        ternary(1, 0, Q, HALF, ALU.min)
         quant_g(1)
+        quant_w(1, 0)
         transposes(2)
-        load_g(8)
+        load_g(7)
         for i in range(4):
             copy_t(2, i, False)
         for b in range(2):
-            for i in range(SIZES[b]):
-                group(b, i, 0, False)
-        ternary(0, 1, 0, Q, ALU.min)
+            for i in range(2):
+                mx(b, i, 0, 0)
+        for b in range(2):
+            for i in range(2):
+                mx(b, i, 0, 1)
+                evacuate(b, i, 0, False)
+            store_half(first[b], 0)
         quant_g(2)
-        ternary(0, 1, Q, HALF, ALU.min)
-        for i in range(4):
-            group(2, i, 0, False)
+        low_v(0, 1)
         transposes(3)
-        ternary(1, 1, 0, HALF, ALU.min)
-        quant_w(0, 1)
-        quant_w(1, 1)
+        load_g(8)
         for i in range(4):
             copy_t(3, i, False)
+        ternary(0, 1, 0, HALF, ALU.subtract)
+        for i in range(4):
+            group(2, i, 0, i == 3)
+            if i % 2 == 1:
+                store_half(first[2] + i - 1, 0)
+        low_v(1, 1)
+        quant_g(3)
+        transposes(4)
+        quant_w(0, 1)
+        for i in range(4):
+            copy_t(4, i, i == 2)
+        ternary(1, 1, 0, Q, ALU.subtract)
+        for i in range(4):
+            group(3, i, 0, False)
+            if i % 2 == 1:
+                store_half(first[3] + i - 1, 0)
+        quant_g(4)
+        ternary(1, 1, Q, HALF, ALU.subtract)
+        quant_w(1, 1)
+        for i in range(4):
+            group(4, i, 0, i % 2 == 0)
+            if i % 2 == 1:
+                store_half(first[4] + i - 1, 0)
         n = 0
         for b in range(HEAD):
+            if b == HEAD - 1:
+                transposes(HEAD)
+                for i in range(4):
+                    copy_t(HEAD, i, i >= 2)
             for i in range(SIZES[b]):
                 group(b, i, 1, n % 2 == 0)
                 n += 1
-                if n == 4:
-                    quant_g(3)
                 if i % 2 == 1:
-                    store(first[b] + i - 1, 0, 2 * N_IN)
+                    store_half(first[b] + i - 1, 1)
+        quant_g(HEAD)
 
         for b in range(HEAD, n_bunch):
             last = b == n_bunch - 1

@@ -140,7 +140,7 @@ def tile_linearbin_t_kernel(tc, x, weight, bias, grad_out, out):
             nc.vector.quantize_mx(out=gq[b][:, PAD:].bitcast(E5X4), scales=gs[b][:], in_=grp[b][:])
 
         def mx(b, i, h, g):
-            if g == 0:
+            if g == 0 and (b, i, h) not in accs:
                 accs[(b, i, h)] = accp.tile([P, HALF], F32, name="acc", tag="acc")
             c0 = (2 * i + g) * P
             nc.tensor.matmul_mx(
@@ -152,6 +152,13 @@ def tile_linearbin_t_kernel(tc, x, weight, bias, grad_out, out):
                 start=(g == 0),
                 stop=(g == 1),
             )
+
+        def warm(b, i, h, n):
+            accs[(b, i, h)] = accp.tile([P, HALF], F32, name="acc", tag="acc")
+            for r in range(n):
+                nc.tensor.matmul(
+                    accs[(b, i, h)][:], lhsT=wraw[0][:, 0, 0, 0:P], rhs=wraw[0][:, 0, 0, 0:HALF], start=True, stop=True
+                )
 
         def evacuate(b, i, h, on_vector):
             t = first[b] + i
@@ -206,8 +213,10 @@ def tile_linearbin_t_kernel(tc, x, weight, bias, grad_out, out):
         ternary(1, 0, Q, HALF, ALU.min)
         quant_g(1)
         quant_w(1, 0)
+        warm(0, 0, 0, 3)
         transposes(2)
         load_g(7)
+        warm(0, 1, 0, 3)
         for i in range(4):
             copy_t(2, i, False)
         for b in range(2):
@@ -236,6 +245,7 @@ def tile_linearbin_t_kernel(tc, x, weight, bias, grad_out, out):
         for i in range(4):
             copy_t(4, i, i == 2)
         ternary(1, 1, 0, Q, ALU.subtract)
+        warm(3, 0, 0, 3)
         for i in range(4):
             group(3, i, 0, False)
             if i % 2 == 1:
@@ -243,6 +253,7 @@ def tile_linearbin_t_kernel(tc, x, weight, bias, grad_out, out):
         quant_g(4)
         ternary(1, 1, Q, HALF, ALU.subtract)
         quant_w(1, 1)
+        warm(4, 0, 0, 4)
         for i in range(4):
             group(4, i, 0, i % 2 == 0)
             if i % 2 == 1:

@@ -21,9 +21,10 @@ BYTES = 2 * N_TOK * N_OUT + 2 * N_OUT * N_IN + 4 * N_TOK * N_IN
 N_TILES = N_TOK // P
 HALF = 512
 SIZES = [2, 2, 4, 4, 4, 4, 4, 4, 4]
+HALVES = 5
 PAD = 48
 FINE = 6
-HEAD = 5
+HEAD = 6
 
 
 def tile_linearbin_t_kernel(tc, x, weight, bias, grad_out, out):
@@ -37,14 +38,17 @@ def tile_linearbin_t_kernel(tc, x, weight, bias, grad_out, out):
         const = ctx.enter_context(tc.tile_pool(name="const", bufs=1))
         grawp = ctx.enter_context(tc.tile_pool(name="grawp", bufs=7))
         grpp = ctx.enter_context(tc.tile_pool(name="grpp", bufs=2))
-        gqp = ctx.enter_context(tc.tile_pool(name="gqp", bufs=6))
-        osp = ctx.enter_context(tc.tile_pool(name="osp", bufs=4))
-        xtp = ctx.enter_context(tc.psum_pool(name="xtp", bufs=4))
-        accp = ctx.enter_context(tc.psum_pool(name="accp", bufs=4))
+        gqp = ctx.enter_context(tc.tile_pool(name="gqp", bufs=7))
+        osp = ctx.enter_context(tc.tile_pool(name="osp", bufs=5))
+        bankp = ctx.enter_context(tc.psum_pool(name="bankp", bufs=8))
         ctx.enter_context(tc.manual_schedule())
 
         ident = const.tile([P, P], F32, name="ident")
         make_identity(nc, ident[:])
+        ident_b = const.tile([P, P], BF16, name="ident_b")
+        make_identity(nc, ident_b[:])
+        pos = const.tile([P, 4, HALF], BF16, name="pos")
+        neg = const.tile([P, 4, HALF], BF16, name="neg")
 
         wraw = [const.tile([P, 2, 2, N_IN], BF16, name="wraw%d" % g) for g in range(2)]
         thr = const.tile([P, 1], F32, name="thr")
@@ -80,16 +84,21 @@ def tile_linearbin_t_kernel(tc, x, weight, bias, grad_out, out):
 
         def load_g(b):
             nt = SIZES[b]
-            graw[b] = grawp.tile([P, nt * N_OUT], BF16, name="graw%d" % nt, tag="graw%d" % nt, bufs=2 if nt == 2 else 5)
+            graw[b] = grawp.tile([P, nt * N_OUT], BF16, name="graw%d" % nt, tag="graw%d" % nt, bufs=2 if nt == 2 else 4)
             nc.sync.dma_start(out=graw[b][:], in_=g_view[:, first[b] * N_OUT : (first[b] + nt) * N_OUT])
 
         def w_view(g, h, c0, c1):
             return wraw[g][:].rearrange("p u e c -> p (u e) c")[:, :, HALF * h + c0 : HALF * h + c1]
 
-        def low_v(g, h):
-            nc.vector.tensor_scalar(
-                out=low[(g, h)][:], in0=w_view(g, h, 0, HALF), scalar1=-THRESHOLD, scalar2=None, op0=ALU.is_lt
-            )
+        def low_v(g, h, us=(0, 1)):
+            for u in us:
+                nc.vector.tensor_scalar(
+                    out=low[(g, h)][:, 2 * u : 2 * u + 2, :],
+                    in0=wraw[g][:, u, :, HALF * h : HALF * (h + 1)],
+                    scalar1=-THRESHOLD,
+                    scalar2=None,
+                    op0=ALU.is_lt,
+                )
 
         def low_s(g, h, c0, c1):
             nc.scalar.activation(
@@ -106,6 +115,33 @@ def tile_linearbin_t_kernel(tc, x, weight, bias, grad_out, out):
                 op1=op1,
             )
 
+        def masks(g, h):
+            for u in range(2):
+                w = wraw[g][:, u, :, HALF * h : HALF * (h + 1)]
+                t = slice(2 * u, 2 * u + 2)
+                nc.vector.tensor_scalar(
+                    out=neg[:, t, :], in0=w, scalar1=-THRESHOLD, scalar2=-1.0, op0=ALU.is_lt, op1=ALU.mult
+                )
+                nc.vector.tensor_scalar(out=pos[:, t, :], in0=w, scalar1=THRESHOLD, scalar2=None, op0=ALU.is_gt)
+
+        def ternary_pe(g, h, q, on_vector):
+            c0 = P * q
+            ps = bankp.tile([P, HALF], F32, name="acc", tag="bank")
+            for m, mask in enumerate((neg, pos)):
+                nc.tensor.matmul(
+                    ps[:],
+                    lhsT=ident_b[:],
+                    rhs=mask[:, :, c0 : c0 + P].rearrange("p t c -> p c t"),
+                    start=(m == 0),
+                    stop=(m == 1),
+                )
+            src = ps[:]
+            dst = wbg[(g, h)][:, c0 : c0 + P, :].rearrange("p c t -> p (c t)")
+            if on_vector:
+                nc.vector.tensor_copy(out=dst, in_=src)
+            else:
+                nc.scalar.copy(out=dst, in_=src)
+
         def quant_w(g, h):
             nc.vector.quantize_mx(
                 out=wq[(g, h)][:].bitcast(E4X4),
@@ -116,7 +152,7 @@ def tile_linearbin_t_kernel(tc, x, weight, bias, grad_out, out):
         def transposes(b):
             g32 = graw[b][:].bitcast(F32)
             for i in range(SIZES[b]):
-                xt = xtp.tile([P, 4, P], F32, name="xt", tag="xt")
+                xt = bankp.tile([P, 4, P], F32, name="xt", tag="bank")
                 for s in range(4):
                     c0 = 512 * i + P * s
                     nc.tensor.transpose(xt[:, s, :], g32[:, c0 : c0 + P], ident[:])
@@ -139,9 +175,9 @@ def tile_linearbin_t_kernel(tc, x, weight, bias, grad_out, out):
             gs[b] = gqp.tile([P, nt * 256], U8, name="gs", tag="gs", align_bytes=256)
             nc.vector.quantize_mx(out=gq[b][:, PAD:].bitcast(E5X4), scales=gs[b][:], in_=grp[b][:])
 
-        def mx(b, i, h, g):
-            if g == 0 and (b, i, h) not in accs:
-                accs[(b, i, h)] = accp.tile([P, HALF], F32, name="acc", tag="acc")
+        def mx(b, i, h, g, begin):
+            if begin:
+                accs[(b, i, h)] = bankp.tile([P, HALF], F32, name="acc", tag="bank")
             c0 = (2 * i + g) * P
             nc.tensor.matmul_mx(
                 out=accs[(b, i, h)][:],
@@ -149,20 +185,13 @@ def tile_linearbin_t_kernel(tc, x, weight, bias, grad_out, out):
                 lhsT_scale=gs[b][:, c0 : c0 + P],
                 rhs=wq[(g, h)][:].bitcast(E4X4),
                 rhs_scale=ws[(g, h)][:],
-                start=(g == 0),
-                stop=(g == 1),
+                start=begin,
+                stop=not begin,
             )
-
-        def warm(b, i, h, n):
-            accs[(b, i, h)] = accp.tile([P, HALF], F32, name="acc", tag="acc")
-            for r in range(n):
-                nc.tensor.matmul(
-                    accs[(b, i, h)][:], lhsT=wraw[0][:, 0, 0, 0:P], rhs=wraw[0][:, 0, 0, 0:HALF], start=True, stop=True
-                )
 
         def evacuate(b, i, h, on_vector):
             t = first[b] + i
-            if b < HEAD:
+            if b < HALVES:
                 if (t // 2, h) not in osth:
                     osth[(t // 2, h)] = osp.tile([P, 2, HALF], F32, name="osth", tag="osth", bufs=12)
                 dst = osth[(t // 2, h)][:, t % 2, :]
@@ -178,8 +207,8 @@ def tile_linearbin_t_kernel(tc, x, weight, bias, grad_out, out):
                 nc.scalar.copy(out=dst, in_=src)
 
         def group(b, i, h, on_vector):
-            mx(b, i, h, 0)
-            mx(b, i, h, 1)
+            mx(b, i, h, 0, True)
+            mx(b, i, h, 1, False)
             evacuate(b, i, h, on_vector)
 
         def store_half(t, h):
@@ -190,86 +219,72 @@ def tile_linearbin_t_kernel(tc, x, weight, bias, grad_out, out):
             nc.sync.dma_start(out=o_view[:, t * N_IN + c0 : t * N_IN + c0 + width], in_=ost[t // 2][:, c0 : c0 + width])
 
         Q = HALF // 2
-        load_w(0, 0)
         load_w(1, 0)
+        load_w(0, 0)
         for b in range(4):
             load_g(b)
         load_w(0, 1)
         load_w(1, 1)
-        for b in range(4, 7):
+        for b in range(4, 6):
             load_g(b)
-        nc.scalar.activation(out=dummy[:], in_=thr[:], func=ACT.Sign)
+        nc.scalar.activation(out=dummy[:], in_=thr[:], func=ACT.Copy)
+        masks(1, 0)
         low_v(0, 0)
         ternary(0, 0, 0, HALF, ALU.subtract)
-        low_s(1, 0, 0, HALF)
-        quant_w(0, 0)
+        for q in range(4):
+            ternary_pe(1, 0, q, False)
         transposes(0)
         transposes(1)
         for b in range(2):
             for i in range(2):
                 copy_t(b, i, False)
-        ternary(1, 0, 0, Q, ALU.min)
-        quant_g(0)
-        ternary(1, 0, Q, HALF, ALU.min)
-        quant_g(1)
         quant_w(1, 0)
-        warm(0, 0, 0, 3)
+        quant_g(0)
+        quant_w(0, 0)
+        quant_g(1)
         transposes(2)
-        load_g(7)
-        warm(0, 1, 0, 3)
+        load_g(6)
         for i in range(4):
             copy_t(2, i, False)
         for b in range(2):
             for i in range(2):
-                mx(b, i, 0, 0)
+                mx(b, i, 0, 1, True)
         for b in range(2):
             for i in range(2):
-                mx(b, i, 0, 1)
+                mx(b, i, 0, 0, False)
                 evacuate(b, i, 0, False)
             store_half(first[b], 0)
         quant_g(2)
-        low_v(0, 1)
-        transposes(3)
-        load_g(8)
-        for i in range(4):
-            copy_t(3, i, False)
-        ternary(0, 1, 0, HALF, ALU.subtract)
-        for i in range(4):
-            group(2, i, 0, i == 3)
-            if i % 2 == 1:
-                store_half(first[2] + i - 1, 0)
-        low_v(1, 1)
-        quant_g(3)
-        transposes(4)
-        quant_w(0, 1)
-        for i in range(4):
-            copy_t(4, i, i == 2)
-        ternary(1, 1, 0, Q, ALU.subtract)
-        warm(3, 0, 0, 3)
-        for i in range(4):
-            group(3, i, 0, False)
-            if i % 2 == 1:
-                store_half(first[3] + i - 1, 0)
-        quant_g(4)
-        ternary(1, 1, Q, HALF, ALU.subtract)
-        quant_w(1, 1)
-        warm(4, 0, 0, 4)
-        for i in range(4):
-            group(4, i, 0, i % 2 == 0)
-            if i % 2 == 1:
-                store_half(first[4] + i - 1, 0)
+        weights_steps = [
+            (lambda: low_v(0, 1), lambda: ternary(0, 1, 0, Q, ALU.subtract)),
+            (lambda: ternary(0, 1, Q, HALF, ALU.subtract), lambda: quant_w(0, 1)),
+            (lambda: low_v(1, 1), lambda: ternary(1, 1, 0, Q, ALU.subtract)),
+            (lambda: ternary(1, 1, Q, HALF, ALU.subtract), lambda: quant_w(1, 1)),
+        ]
+        for b in range(2, HEAD):
+            if b + 1 <= HEAD:
+                transposes(b + 1)
+                if b + 5 < n_bunch:
+                    load_g(b + 5)
+                for i in range(4):
+                    copy_t(b + 1, i, False)
+            for step in weights_steps[b - 2]:
+                step()
+            for i in range(4):
+                group(b, i, 0, i < 1)
+                if b < HALVES and i % 2 == 1:
+                    store_half(first[b] + i - 1, 0)
+            quant_g(b + 1)
         n = 0
         for b in range(HEAD):
-            if b == HEAD - 1:
-                transposes(HEAD)
-                for i in range(4):
-                    copy_t(HEAD, i, i >= 2)
             for i in range(SIZES[b]):
                 group(b, i, 1, n % 2 == 0)
                 n += 1
                 if i % 2 == 1:
-                    store_half(first[b] + i - 1, 1)
-        quant_g(HEAD)
+                    if b < HALVES:
+                        store_half(first[b] + i - 1, 1)
+                    else:
+                        store(first[b] + i - 1, 0, 2 * N_IN)
 
         for b in range(HEAD, n_bunch):
             last = b == n_bunch - 1

@@ -127,16 +127,17 @@ def tile_linearbin_t_kernel(tc, x, weight, bias, grad_out, out):
         def ternary_pe(g, h, q, on_vector):
             c0 = P * q
             ps = bankp.tile([P, HALF], F32, name="acc", tag="bank")
-            for m, mask in enumerate((neg, pos)):
-                nc.tensor.matmul(
-                    ps[:],
-                    lhsT=ident_b[:],
-                    rhs=mask[:, :, c0 : c0 + P].rearrange("p t c -> p c t"),
-                    start=(m == 0),
-                    stop=(m == 1),
-                )
-            src = ps[:]
-            dst = wbg[(g, h)][:, c0 : c0 + P, :].rearrange("p c t -> p (c t)")
+            for t in range(4):
+                for m, mask in enumerate((neg, pos)):
+                    nc.tensor.matmul(
+                        ps[:, P * t : P * (t + 1)],
+                        lhsT=ident_b[:],
+                        rhs=mask[:, t, c0 : c0 + P],
+                        start=(m == 0),
+                        stop=(m == 1),
+                    )
+            src = ps[:].rearrange("p (t c) -> p c t", t=4)
+            dst = wbg[(g, h)][:, c0 : c0 + P, :]
             if on_vector:
                 nc.vector.tensor_copy(out=dst, in_=src)
             else:

@@ -21,10 +21,10 @@ BYTES = 2 * N_TOK * N_OUT + 2 * N_OUT * N_IN + 4 * N_TOK * N_IN
 N_TILES = N_TOK // P
 HALF = 512
 SIZES = [2, 2, 4, 4, 4, 4, 4, 4, 4]
-HALVES = 5
+HALVES = 4
 PAD = 48
-FINE = 6
-HEAD = 6
+FINE = 7
+HEAD = 5
 
 
 def tile_linearbin_t_kernel(tc, x, weight, bias, grad_out, out):
@@ -39,7 +39,7 @@ def tile_linearbin_t_kernel(tc, x, weight, bias, grad_out, out):
         grawp = ctx.enter_context(tc.tile_pool(name="grawp", bufs=7))
         grpp = ctx.enter_context(tc.tile_pool(name="grpp", bufs=2))
         gqp = ctx.enter_context(tc.tile_pool(name="gqp", bufs=7))
-        osp = ctx.enter_context(tc.tile_pool(name="osp", bufs=5))
+        osp = ctx.enter_context(tc.tile_pool(name="osp", bufs=6))
         bankp = ctx.enter_context(tc.psum_pool(name="bankp", bufs=8))
         ctx.enter_context(tc.manual_schedule())
 
@@ -50,7 +50,7 @@ def tile_linearbin_t_kernel(tc, x, weight, bias, grad_out, out):
         pos = const.tile([P, 4, HALF], BF16, name="pos")
         neg = const.tile([P, 4, HALF], BF16, name="neg")
 
-        wraw = [const.tile([P, 2, 2, N_IN], BF16, name="wraw%d" % g) for g in range(2)]
+        wraw = {}
         thr = const.tile([P, 1], F32, name="thr")
         nc.vector.memset(thr[:], THRESHOLD)
         dummy = const.tile([P, 1], F32, name="dummy")
@@ -60,6 +60,7 @@ def tile_linearbin_t_kernel(tc, x, weight, bias, grad_out, out):
         ws = {}
         for g in range(2):
             for h in range(2):
+                wraw[(g, h)] = const.tile([P, 2, 2, HALF], BF16, name="wraw%d%d" % (g, h))
                 low[(g, h)] = const.tile([P, 4, HALF], BF16, name="low%d" % g)
                 wbg[(g, h)] = const.tile([P, HALF, 4], BF16, name="wbg%d" % g, align_bytes=64)
                 wq[(g, h)] = const.tile([P, HALF], U32, name="wq%d%d" % (g, h), align_bytes=256)
@@ -78,7 +79,7 @@ def tile_linearbin_t_kernel(tc, x, weight, bias, grad_out, out):
             for u in range(2):
                 r0 = 512 * g + 256 * u
                 nc.sync.dma_start(
-                    out=wraw[g][:, u, :, HALF * h : HALF * (h + 1)],
+                    out=wraw[(g, h)][:, u, :, :],
                     in_=weight[r0 : r0 + 256, HALF * h : HALF * (h + 1)].rearrange("(q e) c -> q e c", e=2),
                 )
 
@@ -88,13 +89,13 @@ def tile_linearbin_t_kernel(tc, x, weight, bias, grad_out, out):
             nc.sync.dma_start(out=graw[b][:], in_=g_view[:, first[b] * N_OUT : (first[b] + nt) * N_OUT])
 
         def w_view(g, h, c0, c1):
-            return wraw[g][:].rearrange("p u e c -> p (u e) c")[:, :, HALF * h + c0 : HALF * h + c1]
+            return wraw[(g, h)][:].rearrange("p u e c -> p (u e) c")[:, :, c0:c1]
 
         def low_v(g, h, us=(0, 1)):
             for u in us:
                 nc.vector.tensor_scalar(
                     out=low[(g, h)][:, 2 * u : 2 * u + 2, :],
-                    in0=wraw[g][:, u, :, HALF * h : HALF * (h + 1)],
+                    in0=wraw[(g, h)][:, u, :, :],
                     scalar1=-THRESHOLD,
                     scalar2=None,
                     op0=ALU.is_lt,
@@ -117,7 +118,7 @@ def tile_linearbin_t_kernel(tc, x, weight, bias, grad_out, out):
 
         def masks(g, h):
             for u in range(2):
-                w = wraw[g][:, u, :, HALF * h : HALF * (h + 1)]
+                w = wraw[(g, h)][:, u, :, :]
                 t = slice(2 * u, 2 * u + 2)
                 nc.vector.tensor_scalar(
                     out=neg[:, t, :], in0=w, scalar1=-THRESHOLD, scalar2=-1.0, op0=ALU.is_lt, op1=ALU.mult
@@ -194,7 +195,7 @@ def tile_linearbin_t_kernel(tc, x, weight, bias, grad_out, out):
             t = first[b] + i
             if b < HALVES:
                 if (t // 2, h) not in osth:
-                    osth[(t // 2, h)] = osp.tile([P, 2, HALF], F32, name="osth", tag="osth", bufs=12)
+                    osth[(t // 2, h)] = osp.tile([P, 2, HALF], F32, name="osth", tag="osth", bufs=8)
                 dst = osth[(t // 2, h)][:, t % 2, :]
             else:
                 if t // 2 not in ost:
@@ -255,12 +256,12 @@ def tile_linearbin_t_kernel(tc, x, weight, bias, grad_out, out):
                 mx(b, i, 0, 0, False)
                 evacuate(b, i, 0, False)
             store_half(first[b], 0)
+        low_v(0, 1)
         quant_g(2)
         weights_steps = [
-            (lambda: low_v(0, 1), lambda: ternary(0, 1, 0, Q, ALU.subtract)),
-            (lambda: ternary(0, 1, Q, HALF, ALU.subtract), lambda: quant_w(0, 1)),
-            (lambda: low_v(1, 1), lambda: ternary(1, 1, 0, Q, ALU.subtract)),
-            (lambda: ternary(1, 1, Q, HALF, ALU.subtract), lambda: quant_w(1, 1)),
+            (lambda: ternary(0, 1, 0, HALF, ALU.subtract),),
+            (lambda: quant_w(0, 1), lambda: low_v(1, 1)),
+            (lambda: ternary(1, 1, 0, HALF, ALU.subtract), lambda: quant_w(1, 1)),
         ]
         for b in range(2, HEAD):
             if b + 1 <= HEAD:

@@ -229,7 +229,7 @@ def tile_linearbin_t_kernel(tc, x, weight, bias, grad_out, out):
         load_w(1, 1)
         for b in range(4, 6):
             load_g(b)
-        nc.scalar.activation(out=dummy[:], in_=thr[:], func=ACT.Copy)
+        nc.scalar.activation(out=dummy[:], in_=thr[:], func=ACT.Sign)
         masks(1, 0)
         low_v(0, 0)
         ternary(0, 0, 0, HALF, ALU.subtract)
@@ -258,30 +258,45 @@ def tile_linearbin_t_kernel(tc, x, weight, bias, grad_out, out):
             store_half(first[b], 0)
         low_v(0, 1)
         quant_g(2)
-        weights_steps = [
-            (lambda: ternary(0, 1, 0, HALF, ALU.subtract),),
-            (lambda: quant_w(0, 1), lambda: low_v(1, 1)),
-            (lambda: ternary(1, 1, 0, HALF, ALU.subtract), lambda: quant_w(1, 1)),
-        ]
-        for b in range(2, HEAD):
-            if b + 1 <= HEAD:
-                transposes(b + 1)
-                if b + 5 < n_bunch:
-                    load_g(b + 5)
-                for i in range(4):
-                    copy_t(b + 1, i, False)
-            for step in weights_steps[b - 2]:
-                step()
-            for i in range(4):
-                group(b, i, 0, i < 1)
-                if b < HALVES and i % 2 == 1:
-                    store_half(first[b] + i - 1, 0)
-            quant_g(b + 1)
+        transposes(3)
+        load_g(7)
+        for i in range(4):
+            copy_t(3, i, i == 0)
+        ternary(0, 1, 0, HALF, ALU.subtract)
+        for i in range(2):
+            group(2, i, 0, i == 0)
+        store_half(first[2], 0)
+        transposes(4)
+        load_g(8)
+        for i in range(4):
+            copy_t(4, i, False)
+        quant_g(3)
+        quant_w(0, 1)
+        low_v(1, 1)
+        for i in range(2, 4):
+            group(2, i, 0, False)
+        store_half(first[2] + 2, 0)
+        for i in range(4):
+            group(3, i, 0, False)
+            if i % 2 == 1:
+                store_half(first[3] + i - 1, 0)
+        quant_g(4)
+        ternary(1, 1, 0, HALF, ALU.subtract)
+        quant_w(1, 1)
+        transposes(5)
+        for i in range(4):
+            copy_t(5, i, False)
+        for i in range(4):
+            group(4, i, 0, i >= 2)
+            if HALVES > 4 and i % 2 == 1:
+                store_half(first[4] + i - 1, 0)
         n = 0
         for b in range(HEAD):
             for i in range(SIZES[b]):
                 group(b, i, 1, n % 2 == 0)
                 n += 1
+                if n == 8:
+                    quant_g(HEAD)
                 if i % 2 == 1:
                     if b < HALVES:
                         store_half(first[b] + i - 1, 1)

@@ -23,7 +23,7 @@ HALF = 512
 SIZES = [2, 2, 4, 4, 4, 4, 4, 4, 4]
 HALVES = 4
 PAD = 48
-FINE = 7
+FINE = 6
 HEAD = 5
 
 
@@ -39,7 +39,7 @@ def tile_linearbin_t_kernel(tc, x, weight, bias, grad_out, out):
         grawp = ctx.enter_context(tc.tile_pool(name="grawp", bufs=7))
         grpp = ctx.enter_context(tc.tile_pool(name="grpp", bufs=2))
         gqp = ctx.enter_context(tc.tile_pool(name="gqp", bufs=7))
-        osp = ctx.enter_context(tc.tile_pool(name="osp", bufs=6))
+        osp = ctx.enter_context(tc.tile_pool(name="osp", bufs=3))
         bankp = ctx.enter_context(tc.psum_pool(name="bankp", bufs=8))
         ctx.enter_context(tc.manual_schedule())
 
@@ -194,14 +194,14 @@ def tile_linearbin_t_kernel(tc, x, weight, bias, grad_out, out):
         def evacuate(b, i, h, on_vector):
             t = first[b] + i
             if b < HALVES:
-                if (t // 2, h) not in osth:
-                    osth[(t // 2, h)] = osp.tile([P, 2, HALF], F32, name="osth", tag="osth", bufs=8)
-                dst = osth[(t // 2, h)][:, t % 2, :]
+                if (t // 4, h) not in osth:
+                    osth[(t // 4, h)] = osp.tile([P, 4, HALF], F32, name="osth", tag="osth", bufs=4)
+                dst = osth[(t // 4, h)][:, t % 4, :]
             else:
-                if t // 2 not in ost:
-                    ost[t // 2] = osp.tile([P, 2 * N_IN], F32, name="ost", tag="ost")
-                c0 = (t % 2) * N_IN + h * HALF
-                dst = ost[t // 2][:, c0 : c0 + HALF]
+                if t // 4 not in ost:
+                    ost[t // 4] = osp.tile([P, 4 * N_IN], F32, name="ost", tag="ost")
+                c0 = (t % 4) * N_IN + h * HALF
+                dst = ost[t // 4][:, c0 : c0 + HALF]
             src = accs[(b, i, h)][:]
             if on_vector:
                 nc.vector.tensor_copy(out=dst, in_=src)
@@ -214,21 +214,23 @@ def tile_linearbin_t_kernel(tc, x, weight, bias, grad_out, out):
             evacuate(b, i, h, on_vector)
 
         def store_half(t, h):
-            dst = o_view[:, t * N_IN : (t + 2) * N_IN].rearrange("p (t h i) -> p t h i", t=2, h=2)[:, :, h, :]
-            nc.sync.dma_start(out=dst, in_=osth[(t // 2, h)][:])
+            dst = o_view[:, t * N_IN : (t + 4) * N_IN].rearrange("p (t h i) -> p t h i", t=4, h=2)[:, :, h, :]
+            nc.sync.dma_start(out=dst, in_=osth[(t // 4, h)][:])
 
         def store(t, c0, width):
-            nc.sync.dma_start(out=o_view[:, t * N_IN + c0 : t * N_IN + c0 + width], in_=ost[t // 2][:, c0 : c0 + width])
+            s0 = (t % 4) * N_IN + c0
+            nc.sync.dma_start(out=o_view[:, t * N_IN + c0 : t * N_IN + c0 + width], in_=ost[t // 4][:, s0 : s0 + width])
 
         Q = HALF // 2
         load_w(1, 0)
         load_w(0, 0)
-        for b in range(4):
+        for b in range(3):
             load_g(b)
         load_w(0, 1)
+        load_g(3)
+        load_g(4)
         load_w(1, 1)
-        for b in range(4, 6):
-            load_g(b)
+        load_g(5)
         nc.scalar.activation(out=dummy[:], in_=thr[:], func=ACT.Sign)
         masks(1, 0)
         low_v(0, 0)
@@ -255,7 +257,7 @@ def tile_linearbin_t_kernel(tc, x, weight, bias, grad_out, out):
             for i in range(2):
                 mx(b, i, 0, 0, False)
                 evacuate(b, i, 0, False)
-            store_half(first[b], 0)
+        store_half(0, 0)
         low_v(0, 1)
         quant_g(2)
         transposes(3)
@@ -265,7 +267,6 @@ def tile_linearbin_t_kernel(tc, x, weight, bias, grad_out, out):
         ternary(0, 1, 0, HALF, ALU.subtract)
         for i in range(2):
             group(2, i, 0, i == 0)
-        store_half(first[2], 0)
         transposes(4)
         load_g(8)
         for i in range(4):
@@ -275,11 +276,10 @@ def tile_linearbin_t_kernel(tc, x, weight, bias, grad_out, out):
         low_v(1, 1)
         for i in range(2, 4):
             group(2, i, 0, False)
-        store_half(first[2] + 2, 0)
+        store_half(first[2], 0)
         for i in range(4):
             group(3, i, 0, False)
-            if i % 2 == 1:
-                store_half(first[3] + i - 1, 0)
+        store_half(first[3], 0)
         quant_g(4)
         ternary(1, 1, 0, HALF, ALU.subtract)
         quant_w(1, 1)
@@ -288,8 +288,6 @@ def tile_linearbin_t_kernel(tc, x, weight, bias, grad_out, out):
             copy_t(5, i, False)
         for i in range(4):
             group(4, i, 0, i >= 2)
-            if HALVES > 4 and i % 2 == 1:
-                store_half(first[4] + i - 1, 0)
         n = 0
         for b in range(HEAD):
             for i in range(SIZES[b]):
@@ -297,11 +295,12 @@ def tile_linearbin_t_kernel(tc, x, weight, bias, grad_out, out):
                 n += 1
                 if n == 8:
                     quant_g(HEAD)
-                if i % 2 == 1:
+                t = first[b] + i
+                if t % 4 == 3:
                     if b < HALVES:
-                        store_half(first[b] + i - 1, 1)
+                        store_half(t - 3, 1)
                     else:
-                        store(first[b] + i - 1, 0, 2 * N_IN)
+                        store(t - 3, 0, 4 * N_IN)
 
         for b in range(HEAD, n_bunch):
             last = b == n_bunch - 1
@@ -316,9 +315,12 @@ def tile_linearbin_t_kernel(tc, x, weight, bias, grad_out, out):
                 if n == 1 and not last:
                     quant_g(b + 1)
                 if last and i == 3:
-                    store(t - 1, N_IN + h * HALF, HALF)
-                elif b >= FINE:
+                    store(t, h * HALF, HALF)
+                elif b >= FINE + 1:
                     if h == 1:
-                        store(t - t % 2, (t % 2) * N_IN, N_IN)
-                elif n in (3, 7):
-                    store(t - 1, 0, 2 * N_IN)
+                        store(t, 0, N_IN)
+                elif b == FINE:
+                    if n in (3, 7):
+                        store(t - 1, 0, 2 * N_IN)
+                elif n == 7:
+                    store(t - 3, 0, 4 * N_IN)

@@ -23,6 +23,8 @@ HALF = 512
 SIZES = [2, 2, 4, 4, 4, 4, 4, 4, 4]
 HALVES = 4
 PAD = 48
+PAIRED = 6
+RAW_BUFS = {2: 2, 4: 4, 8: 1}
 FINE = 6
 HEAD = 5
 
@@ -38,7 +40,7 @@ def tile_linearbin_t_kernel(tc, x, weight, bias, grad_out, out):
         const = ctx.enter_context(tc.tile_pool(name="const", bufs=1))
         grawp = ctx.enter_context(tc.tile_pool(name="grawp", bufs=7))
         grpp = ctx.enter_context(tc.tile_pool(name="grpp", bufs=2))
-        gqp = ctx.enter_context(tc.tile_pool(name="gqp", bufs=7))
+        gqp = ctx.enter_context(tc.tile_pool(name="gqp", bufs=6))
         osp = ctx.enter_context(tc.tile_pool(name="osp", bufs=3))
         bankp = ctx.enter_context(tc.psum_pool(name="bankp", bufs=8))
         ctx.enter_context(tc.manual_schedule())
@@ -49,19 +51,19 @@ def tile_linearbin_t_kernel(tc, x, weight, bias, grad_out, out):
         make_identity(nc, ident_b[:])
         pos = const.tile([P, 4, HALF], BF16, name="pos")
         neg = const.tile([P, 4, HALF], BF16, name="neg")
+        low0 = const.tile([P, 4, HALF], BF16, name="low0")
 
         wraw = {}
         thr = const.tile([P, 1], F32, name="thr")
         nc.vector.memset(thr[:], THRESHOLD)
         dummy = const.tile([P, 1], F32, name="dummy")
-        low = {}
+        low = {(0, 0): low0, (0, 1): pos, (1, 1): neg}
         wbg = {}
         wq = {}
         ws = {}
         for g in range(2):
             for h in range(2):
                 wraw[(g, h)] = const.tile([P, 2, 2, HALF], BF16, name="wraw%d%d" % (g, h))
-                low[(g, h)] = const.tile([P, 4, HALF], BF16, name="low%d" % g)
                 wbg[(g, h)] = const.tile([P, HALF, 4], BF16, name="wbg%d" % g, align_bytes=64)
                 wq[(g, h)] = const.tile([P, HALF], U32, name="wq%d%d" % (g, h), align_bytes=256)
                 ws[(g, h)] = const.tile([P, HALF], U8, name="ws%d%d" % (g, h), align_bytes=256)
@@ -84,9 +86,12 @@ def tile_linearbin_t_kernel(tc, x, weight, bias, grad_out, out):
                 )
 
         def load_g(b):
-            nt = SIZES[b]
-            graw[b] = grawp.tile([P, nt * N_OUT], BF16, name="graw%d" % nt, tag="graw%d" % nt, bufs=2 if nt == 2 else 4)
-            nc.sync.dma_start(out=graw[b][:], in_=g_view[:, first[b] * N_OUT : (first[b] + nt) * N_OUT])
+            nt = SIZES[b] * (2 if b == PAIRED else 1)
+            raw = grawp.tile([P, nt * N_OUT], BF16, name="graw%d" % nt, tag="graw%d" % nt, bufs=RAW_BUFS[nt])
+            nc.sync.dma_start(out=raw[:], in_=g_view[:, first[b] * N_OUT : (first[b] + nt) * N_OUT])
+            graw[b] = raw[:, 0 : SIZES[b] * N_OUT]
+            if b == PAIRED:
+                graw[b + 1] = raw[:, SIZES[b] * N_OUT : nt * N_OUT]
 
         def w_view(g, h, c0, c1):
             return wraw[(g, h)][:].rearrange("p u e c -> p (u e) c")[:, :, c0:c1]
@@ -152,7 +157,7 @@ def tile_linearbin_t_kernel(tc, x, weight, bias, grad_out, out):
             )
 
         def transposes(b):
-            g32 = graw[b][:].bitcast(F32)
+            g32 = graw[b].bitcast(F32)
             for i in range(SIZES[b]):
                 xt = bankp.tile([P, 4, P], F32, name="xt", tag="bank")
                 for s in range(4):
@@ -231,6 +236,7 @@ def tile_linearbin_t_kernel(tc, x, weight, bias, grad_out, out):
         load_g(4)
         load_w(1, 1)
         load_g(5)
+        load_g(6)
         nc.scalar.activation(out=dummy[:], in_=thr[:], func=ACT.Sign)
         masks(1, 0)
         low_v(0, 0)
@@ -247,7 +253,7 @@ def tile_linearbin_t_kernel(tc, x, weight, bias, grad_out, out):
         quant_w(0, 0)
         quant_g(1)
         transposes(2)
-        load_g(6)
+        load_g(8)
         for i in range(4):
             copy_t(2, i, False)
         for b in range(2):
@@ -261,14 +267,12 @@ def tile_linearbin_t_kernel(tc, x, weight, bias, grad_out, out):
         low_v(0, 1)
         quant_g(2)
         transposes(3)
-        load_g(7)
         for i in range(4):
             copy_t(3, i, i == 0)
         ternary(0, 1, 0, HALF, ALU.subtract)
         for i in range(2):
             group(2, i, 0, i == 0)
         transposes(4)
-        load_g(8)
         for i in range(4):
             copy_t(4, i, False)
         quant_g(3)

from contextlib import ExitStack

import concourse.mybir as mybir
from concourse.masks import make_identity

F32 = mybir.dt.float32
BF16 = mybir.dt.bfloat16
U32 = mybir.dt.uint32
U8 = mybir.dt.uint8
E4X4 = mybir.dt.float8_e4m3fn_x4
E5X4 = mybir.dt.float8_e5m2_x4
ALU = mybir.AluOpType
ACT = mybir.ActivationFunctionType

P = 128
N_TOK, N_OUT, N_IN = 4096, 1024, 1024
THRESHOLD = 0.05
FLOPS = 2 * N_TOK * N_OUT * N_IN
BYTES = 2 * N_TOK * N_OUT + 2 * N_OUT * N_IN + 4 * N_TOK * N_IN

N_TILES = N_TOK // P
HALF = 512
SIZES = [2, 2, 4, 4, 4, 4, 4, 4, 4]
HALVES = 4
PAD = 48
PAIRED = 6
RAW_BUFS = {2: 2, 4: 4, 8: 1}
FINE = 6
HEAD = 5


def tile_linearbin_t_kernel(tc, x, weight, bias, grad_out, out):
    nc = tc.nc
    n_bunch = len(SIZES)
    first = [sum(SIZES[:b]) for b in range(n_bunch)]
    g_view = grad_out.rearrange("(p t) k -> p (t k)", t=N_TILES)
    o_view = out.rearrange("(p t) i -> p (t i)", t=N_TILES)

    with ExitStack() as ctx:
        const = ctx.enter_context(tc.tile_pool(name="const", bufs=1))
        grawp = ctx.enter_context(tc.tile_pool(name="grawp", bufs=7))
        grpp = ctx.enter_context(tc.tile_pool(name="grpp", bufs=2))
        gqp = ctx.enter_context(tc.tile_pool(name="gqp", bufs=6))
        osp = ctx.enter_context(tc.tile_pool(name="osp", bufs=3))
        bankp = ctx.enter_context(tc.psum_pool(name="bankp", bufs=8))
        ctx.enter_context(tc.manual_schedule())

        ident = const.tile([P, P], F32, name="ident")
        make_identity(nc, ident[:])
        ident_b = const.tile([P, P], BF16, name="ident_b")
        make_identity(nc, ident_b[:])
        pos = const.tile([P, 4, HALF], BF16, name="pos")
        neg = const.tile([P, 4, HALF], BF16, name="neg")
        low0 = const.tile([P, 4, HALF], BF16, name="low0")

        wraw = {}
        thr = const.tile([P, 1], F32, name="thr")
        nc.vector.memset(thr[:], THRESHOLD)
        dummy = const.tile([P, 1], F32, name="dummy")
        low = {(0, 0): low0, (0, 1): pos, (1, 1): neg}
        wbg = {}
        wq = {}
        ws = {}
        for g in range(2):
            for h in range(2):
                wraw[(g, h)] = const.tile([P, 2, 2, HALF], BF16, name="wraw%d%d" % (g, h))
                wbg[(g, h)] = const.tile([P, HALF, 4], BF16, name="wbg%d" % g, align_bytes=64)
                wq[(g, h)] = const.tile([P, HALF], U32, name="wq%d%d" % (g, h), align_bytes=256)
                ws[(g, h)] = const.tile([P, HALF], U8, name="ws%d%d" % (g, h), align_bytes=256)

        graw = {}
        grp = {}
        gq = {}
        gs = {}
        xts = {}
        ost = {}
        osth = {}
        accs = {}

        def load_w(g, h):
            for u in range(2):
                r0 = 512 * g + 256 * u
                nc.sync.dma_start(
                    out=wraw[(g, h)][:, u, :, :],
                    in_=weight[r0 : r0 + 256, HALF * h : HALF * (h + 1)].rearrange("(q e) c -> q e c", e=2),
                )

        def load_g(b):
            nt = SIZES[b] * (2 if b == PAIRED else 1)
            raw = grawp.tile([P, nt * N_OUT], BF16, name="graw%d" % nt, tag="graw%d" % nt, bufs=RAW_BUFS[nt])
            nc.sync.dma_start(out=raw[:], in_=g_view[:, first[b] * N_OUT : (first[b] + nt) * N_OUT])
            graw[b] = raw[:, 0 : SIZES[b] * N_OUT]
            if b == PAIRED:
                graw[b + 1] = raw[:, SIZES[b] * N_OUT : nt * N_OUT]

        def w_view(g, h, c0, c1):
            return wraw[(g, h)][:].rearrange("p u e c -> p (u e) c")[:, :, c0:c1]

        def low_v(g, h, us=(0, 1)):
            for u in us:
                nc.vector.tensor_scalar(
                    out=low[(g, h)][:, 2 * u : 2 * u + 2, :],
                    in0=wraw[(g, h)][:, u, :, :],
                    scalar1=-THRESHOLD,
                    scalar2=None,
                    op0=ALU.is_lt,
                )

        def low_s(g, h, c0, c1):
            nc.scalar.activation(
                out=low[(g, h)][:, :, c0:c1], in_=w_view(g, h, c0, c1), func=ACT.Sign, bias=thr[:, 0:1], scale=1.0
            )

        def ternary(g, h, c0, c1, op1):
            nc.vector.scalar_tensor_tensor(
                out=wbg[(g, h)][:, c0:c1, :],
                in0=w_view(g, h, c0, c1).rearrange("p t c -> p c t"),
                scalar=THRESHOLD,
                in1=low[(g, h)][:, :, c0:c1].rearrange("p t c -> p c t"),
                op0=ALU.is_gt,
                op1=op1,
            )

        def masks(g, h):
            for u in range(2):
                w = wraw[(g, h)][:, u, :, :]
                t = slice(2 * u, 2 * u + 2)
                nc.vector.tensor_scalar(
                    out=neg[:, t, :], in0=w, scalar1=-THRESHOLD, scalar2=-1.0, op0=ALU.is_lt, op1=ALU.mult
                )
                nc.vector.tensor_scalar(out=pos[:, t, :], in0=w, scalar1=THRESHOLD, scalar2=None, op0=ALU.is_gt)

        def ternary_pe(g, h, q, on_vector):
            c0 = P * q
            ps = bankp.tile([P, HALF], F32, name="acc", tag="bank")
            for t in range(4):
                for m, mask in enumerate((neg, pos)):
                    nc.tensor.matmul(
                        ps[:, P * t : P * (t + 1)],
                        lhsT=ident_b[:],
                        rhs=mask[:, t, c0 : c0 + P],
                        start=(m == 0),
                        stop=(m == 1),
                    )
            src = ps[:].rearrange("p (t c) -> p c t", t=4)
            dst = wbg[(g, h)][:, c0 : c0 + P, :]
            if on_vector:
                nc.vector.tensor_copy(out=dst, in_=src)
            else:
                nc.scalar.copy(out=dst, in_=src)

        def quant_w(g, h):
            nc.vector.quantize_mx(
                out=wq[(g, h)][:].bitcast(E4X4),
                scales=ws[(g, h)][:],
                in_=wbg[(g, h)][:].rearrange("p c t -> p (c t)"),
            )

        def transposes(b):
            g32 = graw[b].bitcast(F32)
            for i in range(SIZES[b]):
                xt = bankp.tile([P, 4, P], F32, name="xt", tag="bank")
                for s in range(4):
                    c0 = 512 * i + P * s
                    nc.tensor.transpose(xt[:, s, :], g32[:, c0 : c0 + P], ident[:])
                xts[(b, i)] = xt

        def copy_t(b, i, on_vector):
            nt = SIZES[b]
            if i == 0:
                grp[b] = grpp.tile([P, nt * N_OUT], BF16, name="grp", tag="grp", align_bytes=64)
            dst = grp[b][:].bitcast(F32).rearrange("p (i g r u) -> p i g r u", i=nt, g=2, u=2)[:, i]
            src = xts[(b, i)][:].rearrange("p (g u) r -> p g r u", u=2)
            if on_vector:
                nc.vector.tensor_copy(out=dst, in_=src)
            else:
                nc.scalar.copy(out=dst, in_=src)

        def quant_g(b):
            nt = SIZES[b]
            gq[b] = gqp.tile([P, PAD + nt * 256], U32, name="gq", tag="gq", align_bytes=256)
            gs[b] = gqp.tile([P, nt * 256], U8, name="gs", tag="gs", align_bytes=256)
            nc.vector.quantize_mx(out=gq[b][:, PAD:].bitcast(E5X4), scales=gs[b][:], in_=grp[b][:])

        def mx(b, i, h, g, begin):
            if begin:
                accs[(b, i, h)] = bankp.tile([P, HALF], F32, name="acc", tag="bank")
            c0 = (2 * i + g) * P
            nc.tensor.matmul_mx(
                out=accs[(b, i, h)][:],
                lhsT=gq[b][:, PAD + c0 : PAD + c0 + P].bitcast(E5X4),
                lhsT_scale=gs[b][:, c0 : c0 + P],
                rhs=wq[(g, h)][:].bitcast(E4X4),
                rhs_scale=ws[(g, h)][:],
                start=begin,
                stop=not begin,
            )

        def evacuate(b, i, h, on_vector):
            t = first[b] + i
            if b < HALVES:
                if (t // 4, h) not in osth:
                    osth[(t // 4, h)] = osp.tile([P, 4, HALF], F32, name="osth", tag="osth", bufs=4)
                dst = osth[(t // 4, h)][:, t % 4, :]
            else:
                if t // 4 not in ost:
                    ost[t // 4] = osp.tile([P, 4 * N_IN], F32, name="ost", tag="ost")
                c0 = (t % 4) * N_IN + h * HALF
                dst = ost[t // 4][:, c0 : c0 + HALF]
            src = accs[(b, i, h)][:]
            if on_vector:
                nc.vector.tensor_copy(out=dst, in_=src)
            else:
                nc.scalar.copy(out=dst, in_=src)

        def group(b, i, h, on_vector):
            mx(b, i, h, 0, True)
            mx(b, i, h, 1, False)
            evacuate(b, i, h, on_vector)

        def store_half(t, h):
            dst = o_view[:, t * N_IN : (t + 4) * N_IN].rearrange("p (t h i) -> p t h i", t=4, h=2)[:, :, h, :]
            nc.sync.dma_start(out=dst, in_=osth[(t // 4, h)][:])

        def store(t, c0, width):
            s0 = (t % 4) * N_IN + c0
            nc.sync.dma_start(out=o_view[:, t * N_IN + c0 : t * N_IN + c0 + width], in_=ost[t // 4][:, s0 : s0 + width])

        Q = HALF // 2
        load_w(1, 0)
        load_w(0, 0)
        for b in range(3):
            load_g(b)
        load_w(0, 1)
        load_g(3)
        load_g(4)
        load_w(1, 1)
        load_g(5)
        load_g(6)
        nc.scalar.activation(out=dummy[:], in_=thr[:], func=ACT.Sign)
        masks(1, 0)
        low_v(0, 0)
        ternary(0, 0, 0, HALF, ALU.subtract)
        for q in range(4):
            ternary_pe(1, 0, q, False)
        transposes(0)
        transposes(1)
        for b in range(2):
            for i in range(2):
                copy_t(b, i, False)
        quant_w(1, 0)
        quant_g(0)
        quant_w(0, 0)
        quant_g(1)
        transposes(2)
        load_g(8)
        for i in range(4):
            copy_t(2, i, False)
        for b in range(2):
            for i in range(2):
                mx(b, i, 0, 1, True)
        for b in range(2):
            for i in range(2):
                mx(b, i, 0, 0, False)
                evacuate(b, i, 0, False)
        store_half(0, 0)
        low_v(0, 1)
        quant_g(2)
        transposes(3)
        for i in range(4):
            copy_t(3, i, i == 0)
        ternary(0, 1, 0, HALF, ALU.subtract)
        for i in range(2):
            group(2, i, 0, i == 0)
        transposes(4)
        for i in range(4):
            copy_t(4, i, False)
        quant_g(3)
        quant_w(0, 1)
        low_v(1, 1)
        for i in range(2, 4):
            group(2, i, 0, False)
        store_half(first[2], 0)
        for i in range(4):
            group(3, i, 0, False)
        store_half(first[3], 0)
        quant_g(4)
        ternary(1, 1, 0, HALF, ALU.subtract)
        quant_w(1, 1)
        transposes(5)
        for i in range(4):
            copy_t(5, i, False)
        for i in range(4):
            group(4, i, 0, i >= 2)
        n = 0
        for b in range(HEAD):
            for i in range(SIZES[b]):
                group(b, i, 1, n % 2 == 0)
                n += 1
                if n == 8:
                    quant_g(HEAD)
                t = first[b] + i
                if t % 4 == 3:
                    if b < HALVES:
                        store_half(t - 3, 1)
                    else:
                        store(t - 3, 0, 4 * N_IN)

        for b in range(HEAD, n_bunch):
            last = b == n_bunch - 1
            if not last:
                transposes(b + 1)
                for i in range(4):
                    copy_t(b + 1, i, i >= 2)
            for n in range(8):
                i, h = divmod(n, 2)
                t = first[b] + i
                group(b, i, h, n % 2 == 1 if last else n in (0, 3, 7))
                if n == 1 and not last:
                    quant_g(b + 1)
                if last and i == 3:
                    store(t, h * HALF, HALF)
                elif b >= FINE + 1:
                    if h == 1:
                        store(t, 0, N_IN)
                elif b == FINE:
                    if n in (3, 7):
                        store(t - 1, 0, 2 * N_IN)
                elif n == 7:
                    store(t - 3, 0, 4 * N_IN)
